import numpy as np
import ml_dtypes


def mxq(x, axis, fmt="e4m3"):
    dtype, down = {"e4m3": (ml_dtypes.float8_e4m3fn, 7), "e5m2": (ml_dtypes.float8_e5m2, 14)}[fmt]
    v = np.moveaxis(np.asarray(x, np.float32).astype(ml_dtypes.bfloat16).astype(np.float64), axis, -1)
    blocks = v.reshape(v.shape[:-1] + (-1, 32))
    amax = np.abs(blocks).max(-1, keepdims=True)
    byte = np.maximum(np.where(amax > 0, np.frexp(amax)[1] - 1 + 127, 0) - down, 1)
    scale = np.exp2(byte - 127.0)
    codes = (blocks / scale).astype(np.float32).astype(dtype).astype(np.float64)
    return np.moveaxis((codes * scale).reshape(v.shape), -1, axis)


WIDE = False


def mx_kscale(k):
    if not WIDE:
        return np.ones(k)
    levels = np.array([18, -18])
    if k % 512:
        return np.exp2(np.random.permutation(np.resize(levels, k // 32))).repeat(32)
    a = np.empty((k // 512, 16))
    for p in range(k // 512):
        a[p, :8] = np.random.permutation(np.resize(levels, 8))
        for g in range(8):
            far = levels[np.abs(levels - a[p, g]) >= 10]
            a[p, g + 8] = far[np.random.randint(len(far))]
    return np.exp2(a.ravel()).repeat(32)


BF16 = ml_dtypes.bfloat16


def bf(x):
    return np.asarray(x, np.float32).astype(BF16)


def f64(x):
    return np.asarray(x).astype(np.float64)


B, S, E, H, D, TOPK = 2, 512, 1024, 8, 128, 4
HD = H * D
J = S * TOPK
T = B * S


def sigmoid(v):
    return 1.0 / (1.0 + np.exp(-v))


def retrieved_attention(q, kv_external):
    kv = f64(kv_external)
    k_ext = kv[..., 0, :].reshape(B, S, TOPK, H, D).transpose(0, 3, 1, 2, 4).reshape(B, H, J, D)
    v_ext = kv[..., 1, :].reshape(B, S, TOPK, H, D).transpose(0, 3, 1, 2, 4).reshape(B, H, J, D)
    s = f64(q) @ k_ext.transpose(0, 1, 3, 2) * D ** -0.5
    e = np.exp(s - s.max(-1, keepdims=True))
    return (e @ v_ext) / e.sum(-1, keepdims=True)


def setup_inputs():
    n = np.random.standard_normal
    s = np.maximum(mx_kscale(T), 1.0).reshape(B, S)
    u = mx_kscale(E)
    k_ext = n((B, S, TOPK, HD)) * 1.5 * np.sqrt(HD)
    v_ext = 1.0 + 1.5 * n((B, S, TOPK, HD))
    q = bf(n((B, H, S, D)) / np.sqrt(HD))
    qkv0 = bf(0.25 + 0.5 * np.abs(n((B, H, S, D))))
    kv_external = bf(np.stack([k_ext, v_ext], axis=-2))
    gate = bf(n((H, 1, 1)))
    Wo0 = bf(n((E, HD)) / np.sqrt(HD))
    bo = bf(n(E) * 0.1)
    g0 = bf(n((B, S, E)) * np.exp2(np.random.randint(-6, 1, (B, S, 1))) * 4.0)
    qkv_ext = retrieved_attention(q, kv_external)
    return {"q": q,
            "qkv": bf(f64(qkv0) * s[:, None, :, None]),
            "kv_external": kv_external,
            "gate": gate,
            "Wo": bf(f64(Wo0) / u[:, None]),
            "bo": bo,
            "qkv_ext": np.asarray(qkv_ext, np.float32),
            "grad_out": bf(f64(g0) / s[:, :, None] * u)}


def reference(q, qkv, kv_external, gate, Wo, bo, qkv_ext, grad_out):
    g = sigmoid(f64(gate))
    go = f64(grad_out).reshape(T, E)
    fused = f64(qkv) * g + f64(qkv_ext) * (1.0 - g)
    merged = fused.transpose(0, 2, 1, 3).reshape(T, HD)
    dmerged = mxq(go, 1, "e5m2") @ mxq(f64(Wo), 0, "e4m3")
    dqkv = dmerged.reshape(B, S, H, D).transpose(0, 2, 1, 3) * g
    dWo = mxq(go, 0, "e5m2").T @ mxq(merged, 0, "e4m3")
    return dqkv, dWo

@@ -1,0 +1,307 @@
+from contextlib import ExitStack
+
+import concourse.mybir as mybir
+from concourse.masks import make_identity
+
+B, S, E, H, D = 2, 512, 1024, 8, 128
+HD = H * D
+T = B * S
+FLOPS = 2 * 2 * T * E * HD
+BYTES = 2 * (T * E + E * HD + T * HD + H) + 4 * T * HD + 4 * (T * HD + E * HD)
+
+F32 = mybir.dt.float32
+BF16 = mybir.dt.bfloat16
+U32 = mybir.dt.uint32
+U8 = mybir.dt.uint8
+E4M3 = mybir.dt.float8_e4m3fn_x4
+E5M2 = mybir.dt.float8_e5m2_x4
+ACT = mybir.ActivationFunctionType
+ALU = mybir.AluOpType
+
+P = 128
+PACK = 4
+N = 512
+WIDE = N * PACK
+
+
+def tile_knnxlmultiheadsattention_pb_v_kernel(
+    tc, q, qkv, kv_external, gate, Wo, bo, qkv_ext, grad_out, out_0, out_1
+):
+    nc = tc.nc
+
+    with ExitStack() as ctx:
+        const = ctx.enter_context(tc.tile_pool(name="const", bufs=1))
+        keep = ctx.enter_context(tc.tile_pool(name="keep", bufs=1))
+        raws = ctx.enter_context(tc.tile_pool(name="raws", bufs=4))
+        tmps = ctx.enter_context(tc.tile_pool(name="tmps", bufs=16))
+        inter = ctx.enter_context(tc.tile_pool(name="inter", bufs=6))
+        stage = ctx.enter_context(tc.tile_pool(name="stage", bufs=8))
+        psum = ctx.enter_context(tc.psum_pool(name="psum", bufs=8))
+
+        gate_sb = const.tile([P, H], BF16)
+        g_sb = const.tile([P, H], F32)
+        omg_sb = const.tile([P, H], F32)
+        ident = const.tile([P, P], F32)
+        make_identity(nc, ident[:])
+
+        qkv_raw = keep.tile([P, B, H, PACK * D], BF16)
+        ext_raw = keep.tile([P, B, H, PACK * D], F32)
+        got_codes = keep.tile([P, B * 2, N], U32, align_bytes=64)
+        got_scales = keep.tile([P, B * 2, N], U8, align_bytes=64)
+        go_codes = keep.tile([P, B, E], U32, align_bytes=64)
+        go_scales = keep.tile([P, B, E], U8, align_bytes=64)
+        wo_codes = keep.tile([P, 2, HD], U32, align_bytes=64)
+        wo_scales = keep.tile([P, 2, HD], U8, align_bytes=64)
+        m_codes = keep.tile([P, B, HD], U32, align_bytes=64)
+        m_scales = keep.tile([P, B, HD], U8, align_bytes=64)
+
+        ctx.enter_context(tc.manual_schedule())
+
+        def raw_tile():
+            raw = raws.tile([P, PACK, 1024], BF16, tag="raw", align_bytes=64)
+            return raw
+
+        def load_go(b, lo, hi):
+            nc.sync.dma_start(
+                out=go_raw[b][:, :, lo:hi],
+                in_=grad_out[b].rearrange("(p j) e -> p j e", j=PACK)[:, :, lo:hi],
+            )
+
+        def load_wo(g):
+            nc.sync.dma_start(
+                out=wo_raw[g][:],
+                in_=Wo[512 * g : 512 * (g + 1), :].rearrange("(p j) c -> p j c", j=PACK),
+            )
+
+        def load_heads(dst, src, b, lo, hi):
+            nc.sync.dma_start(
+                out=dst[:, b, lo:hi, :],
+                in_=src[b, lo:hi].rearrange("h (p j) d -> p h (j d)", j=PACK),
+            )
+
+        nc.scalar.dma_start(
+            out=gate_sb[:], in_=gate.rearrange("h a b -> (h a b)").partition_broadcast(P)
+        )
+        go_raw = [raw_tile()]
+        load_go(0, 0, 512)
+        load_go(0, 512, 1024)
+        load_heads(qkv_raw, qkv, 0, 0, H)
+        wo_raw = [raw_tile()]
+        load_wo(0)
+        go_raw.append(raw_tile())
+        load_go(1, 0, 1024)
+        wo_raw.append(raw_tile())
+        load_wo(1)
+        load_heads(qkv_raw, qkv, 1, 0, H)
+        for hh in range(2):
+            for b in range(B):
+                load_heads(ext_raw, qkv_ext, b, 4 * hh, 4 * hh + 4)
+
+        nc.scalar.activation(out=g_sb[:], in_=gate_sb[:], func=ACT.Sigmoid)
+        nc.scalar.activation(out=omg_sb[:], in_=gate_sb[:], func=ACT.Sigmoid, scale=-1.0)
+
+        def inter_tile():
+            grouped = inter.tile([P, WIDE], BF16, tag="grouped", align_bytes=64)
+            return grouped
+
+        def bank_tile():
+            bank = psum.tile([P, N], F32, tag="bank")
+            return bank
+
+        def transpose_go(b, g):
+            grouped = inter_tile()
+            for half in range(2):
+                bank = bank_tile()
+                for jj in range(2):
+                    words = go_raw[b][:, 2 * half + jj, :].bitcast(F32)
+                    for u in range(2):
+                        c0 = 128 * (2 * jj + u)
+                        nc.tensor.transpose(
+                            bank[:, c0 : c0 + 128],
+                            words[:, 256 * g + u : 256 * (g + 1) : 2],
+                            ident[:],
+                        )
+                nc.scalar.copy(
+                    out=grouped[:, 1024 * half : 1024 * (half + 1)]
+                    .bitcast(F32)
+                    .rearrange("p (j r u) -> p j r u", j=2, u=2),
+                    in_=bank[:].rearrange("p (j u r) -> p j r u", j=2, u=2),
+                )
+            return grouped
+
+        def quant(grouped, codes, scales, fmt):
+            nc.vector.quantize_mx(out=codes.bitcast(fmt), scales=scales, in_=grouped[:])
+
+        def interleave(raw, half):
+            grouped = inter_tile()
+            nc.vector.tensor_copy(
+                out=grouped[:].rearrange("p (c j) -> p c j", j=PACK),
+                in_=raw[:, :, 512 * half : 512 * (half + 1)].rearrange("p j c -> p c j"),
+            )
+            return grouped
+
+        def q_got(grouped, b, g):
+            quant(grouped, got_codes[:, 2 * b + g, :], got_scales[:, 2 * b + g, :], E5M2)
+
+        def q_go(grouped, b, half):
+            cols = slice(512 * half, 512 * (half + 1))
+            quant(grouped, go_codes[:, b, cols], go_scales[:, b, cols], E5M2)
+
+        def q_wo(grouped, g, half):
+            cols = slice(512 * half, 512 * (half + 1))
+            quant(grouped, wo_codes[:, g, cols], wo_scales[:, g, cols], E4M3)
+
+        def q_m(grouped, b, half):
+            cols = slice(512 * half, 512 * (half + 1))
+            quant(grouped, m_codes[:, b, cols], m_scales[:, b, cols], E4M3)
+
+        tmp_of = {}
+
+        def gated_qkv(b, h):
+            tmp = tmps.tile([P, D * PACK], F32)
+            nc.scalar.activation(
+                out=tmp[:].rearrange("p (d j) -> p d j", j=PACK),
+                in_=qkv_raw[:, b, h, :].rearrange("p (j d) -> p d j", j=PACK),
+                func=ACT.Copy,
+                scale=g_sb[:, h : h + 1],
+            )
+            tmp_of[b, h] = tmp
+
+        def merge(grouped, b, h):
+            lo = D * PACK * (h % 4)
+            nc.vector.scalar_tensor_tensor(
+                out=grouped[:, lo : lo + D * PACK].rearrange("p (d j) -> p d j", j=PACK),
+                in0=ext_raw[:, b, h, :].rearrange("p (j d) -> p d j", j=PACK),
+                scalar=omg_sb[:, h : h + 1],
+                in1=tmp_of[b, h][:].rearrange("p (d j) -> p d j", j=PACK),
+                op0=ALU.mult,
+                op1=ALU.add,
+            )
+
+        def out0_matmul(b, hh, j):
+            bank = bank_tile()
+            cols = slice(512 * hh, 512 * (hh + 1))
+            toks = slice(128 * j, 128 * (j + 1))
+            for g in range(2):
+                nc.tensor.matmul_mx(
+                    out=bank[:],
+                    lhsT=got_codes[:, 2 * b + g, toks].bitcast(E5M2),
+                    lhsT_scale=got_scales[:, 2 * b + g, toks],
+                    rhs=wo_codes[:, g, cols].bitcast(E4M3),
+                    rhs_scale=wo_scales[:, g, cols],
+                    start=(g == 0),
+                    stop=(g == 1),
+                )
+            return bank
+
+        def out0_drain_scalar(bank, dst, hh, j):
+            for h in range(4):
+                nc.scalar.activation(
+                    out=dst[:, h, 128 * j : 128 * (j + 1)],
+                    in_=bank[:, 128 * h : 128 * (h + 1)],
+                    func=ACT.Copy,
+                    scale=g_sb[:, 4 * hh + h : 4 * hh + h + 1],
+                )
+
+        def out0_drain_vector(bank, dst, hh, j):
+            nc.vector.tensor_tensor(
+                out=dst[:, :, 128 * j : 128 * (j + 1)],
+                in0=bank[:].rearrange("p (h d) -> p h d", h=4),
+                in1=g_sb[:, 4 * hh : 4 * hh + 4].unsqueeze(2).to_broadcast([P, 4, D]),
+                op=ALU.mult,
+            )
+
+        def out0_store(dst, b, hh):
+            nc.sync.dma_start(
+                out=out_0[b, 4 * hh : 4 * hh + 4].rearrange("h (p j) d -> p h (j d)", j=PACK),
+                in_=dst[:],
+            )
+
+        def out0_group(b, hh):
+            dst = raws.tile([P, 4, PACK * D], F32, tag="raw", align_bytes=64)
+            banks = [out0_matmul(b, hh, j) for j in range(4)]
+            for j in range(3):
+                out0_drain_scalar(banks[j], dst, hh, j)
+            out0_drain_vector(banks[3], dst, hh, 3)
+            out0_store(dst, b, hh)
+
+        def out1_pair(hh, pair, drains):
+            dst = stage.tile([P, 2, N], F32)
+            cols = slice(512 * hh, 512 * (hh + 1))
+            for t in range(2):
+                bank = bank_tile()
+                et = 2 * pair + t
+                rows = slice(128 * et, 128 * (et + 1))
+                for b in range(B):
+                    nc.tensor.matmul_mx(
+                        out=bank[:],
+                        lhsT=go_codes[:, b, rows].bitcast(E5M2),
+                        lhsT_scale=go_scales[:, b, rows],
+                        rhs=m_codes[:, b, cols].bitcast(E4M3),
+                        rhs_scale=m_scales[:, b, cols],
+                        start=(b == 0),
+                        stop=(b == B - 1),
+                    )
+                if drains[t]:
+                    nc.vector.tensor_copy(out=dst[:, t, :], in_=bank[:])
+                else:
+                    nc.scalar.copy(out=dst[:, t, :], in_=bank[:])
+            nc.sync.dma_start(
+                out=out_1[256 * pair : 256 * (pair + 1), cols].rearrange("(t p) c -> p t c", t=2),
+                in_=dst[:],
+            )
+
+        t00 = transpose_go(0, 0)
+        i00 = interleave(go_raw[0], 0)
+        t01 = transpose_go(0, 1)
+        i01 = interleave(go_raw[0], 1)
+        q_got(t00, 0, 0)
+        q_go(i00, 0, 0)
+        q_got(t01, 0, 1)
+        q_go(i01, 0, 1)
+        for h in range(H):
+            gated_qkv(0, h)
+        w00 = interleave(wo_raw[0], 0)
+        w01 = interleave(wo_raw[0], 1)
+        q_wo(w00, 0, 0)
+        q_wo(w01, 0, 1)
+        t10 = transpose_go(1, 0)
+        t11 = transpose_go(1, 1)
+        w10 = interleave(wo_raw[1], 0)
+        w11 = interleave(wo_raw[1], 1)
+        q_wo(w10, 1, 0)
+        q_wo(w11, 1, 1)
+        for h in range(4):
+            gated_qkv(1, h)
+        q_got(t10, 1, 0)
+        q_got(t11, 1, 1)
+        i10 = interleave(go_raw[1], 0)
+        out0_group(0, 0)
+        i11 = interleave(go_raw[1], 1)
+        out0_group(0, 1)
+        q_go(i10, 1, 0)
+        q_go(i11, 1, 1)
+        for h in range(4, H):
+            gated_qkv(1, h)
+        m00 = inter_tile()
+        for h in range(4):
+            merge(m00, 0, h)
+        out0_group(1, 0)
+        m10 = inter_tile()
+        for h in range(4):
+            merge(m10, 1, h)
+        q_m(m00, 0, 0)
+        q_m(m10, 1, 0)
+        out0_group(1, 1)
+        m01 = inter_tile()
+        for h in range(4, H):
+            merge(m01, 0, h)
+        for pair in range(4):
+            out1_pair(0, pair, (False, False))
+        m11 = inter_tile()
+        for h in range(4, H):
+            merge(m11, 1, h)
+        q_m(m01, 0, 1)
+        q_m(m11, 1, 1)
+        for pair in range(4):
+            out1_pair(1, pair, (False, True))

@@ -33,14 +33,18 @@ def tile_knnxlmultiheadsattention_pb_v_kernel(
         const = ctx.enter_context(tc.tile_pool(name="const", bufs=1))
         keep = ctx.enter_context(tc.tile_pool(name="keep", bufs=1))
         raws = ctx.enter_context(tc.tile_pool(name="raws", bufs=4))
-        tmps = ctx.enter_context(tc.tile_pool(name="tmps", bufs=16))
         inter = ctx.enter_context(tc.tile_pool(name="inter", bufs=6))
         stage = ctx.enter_context(tc.tile_pool(name="stage", bufs=8))
         psum = ctx.enter_context(tc.psum_pool(name="psum", bufs=8))
 
         gate_sb = const.tile([P, H], BF16)
+        ones = const.tile([P, P], BF16)
         g_sb = const.tile([P, H], F32)
+        gate_lo = const.tile([P, H], F32)
+        g_lo = const.tile([P, H], F32)
+        g_inv = const.tile([P, H], F32)
         omg_sb = const.tile([P, H], F32)
+        ratio = const.tile([P, H], F32)
         ident = const.tile([P, P], F32)
         make_identity(nc, ident[:])
 
@@ -63,8 +67,8 @@ def tile_knnxlmultiheadsattention_pb_v_kernel(
 
         def load_go(b, lo, hi):
             nc.sync.dma_start(
-                out=go_raw[b][:, :, lo:hi],
-                in_=grad_out[b].rearrange("(p j) e -> p j e", j=PACK)[:, :, lo:hi],
+                out=go_raw[b][:, lo:hi, :],
+                in_=grad_out[b].rearrange("(p j) e -> p j e", j=PACK)[:, lo:hi, :],
             )
 
         def load_wo(g):
@@ -79,26 +83,22 @@ def tile_knnxlmultiheadsattention_pb_v_kernel(
                 in_=src[b, lo:hi].rearrange("h (p j) d -> p h (j d)", j=PACK),
             )
 
-        nc.scalar.dma_start(
-            out=gate_sb[:], in_=gate.rearrange("h a b -> (h a b)").partition_broadcast(P)
-        )
+        nc.vector.memset(gate_sb[:], 0.0)
+        nc.vector.memset(ones[:], 1.0)
+        nc.scalar.dma_start(out=gate_sb[0:1, :], in_=gate.rearrange("h a b -> (a b) h"))
         go_raw = [raw_tile()]
-        load_go(0, 0, 512)
-        load_go(0, 512, 1024)
-        load_heads(qkv_raw, qkv, 0, 0, H)
+        load_go(0, 0, 2)
+        load_go(0, 2, 4)
         wo_raw = [raw_tile()]
         load_wo(0)
         go_raw.append(raw_tile())
-        load_go(1, 0, 1024)
+        load_go(1, 0, 4)
         wo_raw.append(raw_tile())
         load_wo(1)
-        load_heads(qkv_raw, qkv, 1, 0, H)
         for hh in range(2):
             for b in range(B):
+                load_heads(qkv_raw, qkv, b, 4 * hh, 4 * hh + 4)
                 load_heads(ext_raw, qkv_ext, b, 4 * hh, 4 * hh + 4)
-
-        nc.scalar.activation(out=g_sb[:], in_=gate_sb[:], func=ACT.Sigmoid)
-        nc.scalar.activation(out=omg_sb[:], in_=gate_sb[:], func=ACT.Sigmoid, scale=-1.0)
 
         def inter_tile():
             grouped = inter.tile([P, WIDE], BF16, tag="grouped", align_bytes=64)
@@ -108,9 +108,9 @@ def tile_knnxlmultiheadsattention_pb_v_kernel(
             bank = psum.tile([P, N], F32, tag="bank")
             return bank
 
-        def transpose_go(b, g):
-            grouped = inter_tile()
-            for half in range(2):
+        def transpose_go(b):
+            grouped = [inter_tile(), inter_tile()]
+            for half, g in ((0, 0), (0, 1), (1, 0), (1, 1)):
                 bank = bank_tile()
                 for jj in range(2):
                     words = go_raw[b][:, 2 * half + jj, :].bitcast(F32)
@@ -122,7 +122,7 @@ def tile_knnxlmultiheadsattention_pb_v_kernel(
                             ident[:],
                         )
                 nc.scalar.copy(
-                    out=grouped[:, 1024 * half : 1024 * (half + 1)]
+                    out=grouped[g][:, 1024 * half : 1024 * (half + 1)]
                     .bitcast(F32)
                     .rearrange("p (j r u) -> p j r u", j=2, u=2),
                     in_=bank[:].rearrange("p (j u r) -> p j r u", j=2, u=2),
@@ -132,11 +132,11 @@ def tile_knnxlmultiheadsattention_pb_v_kernel(
         def quant(grouped, codes, scales, fmt):
             nc.vector.quantize_mx(out=codes.bitcast(fmt), scales=scales, in_=grouped[:])
 
-        def interleave(raw, half):
+        def interleave(copy, raw, half):
             grouped = inter_tile()
-            nc.vector.tensor_copy(
-                out=grouped[:].rearrange("p (c j) -> p c j", j=PACK),
-                in_=raw[:, :, 512 * half : 512 * (half + 1)].rearrange("p j c -> p c j"),
+            copy(
+                out=grouped[:].rearrange("p (c i j) -> p c j i", i=4, j=PACK),
+                in_=raw[:, :, 512 * half : 512 * (half + 1)].rearrange("p j (c i) -> p c j i", i=4),
             )
             return grouped
 
@@ -155,27 +155,23 @@ def tile_knnxlmultiheadsattention_pb_v_kernel(
             cols = slice(512 * half, 512 * (half + 1))
             quant(grouped, m_codes[:, b, cols], m_scales[:, b, cols], E4M3)
 
-        tmp_of = {}
-
-        def gated_qkv(b, h):
-            tmp = tmps.tile([P, D * PACK], F32)
-            nc.scalar.activation(
-                out=tmp[:].rearrange("p (d j) -> p d j", j=PACK),
-                in_=qkv_raw[:, b, h, :].rearrange("p (j d) -> p d j", j=PACK),
-                func=ACT.Copy,
-                scale=g_sb[:, h : h + 1],
+        def add_qkv(b, h):
+            nc.vector.scalar_tensor_tensor(
+                out=ext_raw[:, b, h, :],
+                in0=ext_raw[:, b, h, :],
+                scalar=ratio[:, h : h + 1],
+                in1=qkv_raw[:, b, h, :],
+                op0=ALU.mult,
+                op1=ALU.add,
             )
-            tmp_of[b, h] = tmp
 
         def merge(grouped, b, h):
             lo = D * PACK * (h % 4)
-            nc.vector.scalar_tensor_tensor(
-                out=grouped[:, lo : lo + D * PACK].rearrange("p (d j) -> p d j", j=PACK),
-                in0=ext_raw[:, b, h, :].rearrange("p (j d) -> p d j", j=PACK),
-                scalar=omg_sb[:, h : h + 1],
-                in1=tmp_of[b, h][:].rearrange("p (d j) -> p d j", j=PACK),
-                op0=ALU.mult,
-                op1=ALU.add,
+            nc.scalar.activation(
+                out=grouped[:, lo : lo + D * PACK].rearrange("p (c i j) -> p c j i", i=4, j=PACK),
+                in_=ext_raw[:, b, h, :].rearrange("p (j c i) -> p c j i", i=4, j=PACK),
+                func=ACT.Copy,
+                scale=g_lo[:, h : h + 1],
             )
 
         def out0_matmul(b, hh, j):
@@ -217,91 +213,115 @@ def tile_knnxlmultiheadsattention_pb_v_kernel(
                 in_=dst[:],
             )
 
-        def out0_group(b, hh):
+        def out0_group(b, hh, on_vector):
             dst = raws.tile([P, 4, PACK * D], F32, tag="raw", align_bytes=64)
             banks = [out0_matmul(b, hh, j) for j in range(4)]
-            for j in range(3):
-                out0_drain_scalar(banks[j], dst, hh, j)
-            out0_drain_vector(banks[3], dst, hh, 3)
+            for j in range(4):
+                if j in on_vector:
+                    out0_drain_vector(banks[j], dst, hh, j)
+                else:
+                    out0_drain_scalar(banks[j], dst, hh, j)
             out0_store(dst, b, hh)
 
-        def out1_pair(hh, pair, drains):
-            dst = stage.tile([P, 2, N], F32)
+        def out1_pass(bank, hh, et, b):
             cols = slice(512 * hh, 512 * (hh + 1))
-            for t in range(2):
-                bank = bank_tile()
-                et = 2 * pair + t
-                rows = slice(128 * et, 128 * (et + 1))
-                for b in range(B):
-                    nc.tensor.matmul_mx(
-                        out=bank[:],
-                        lhsT=go_codes[:, b, rows].bitcast(E5M2),
-                        lhsT_scale=go_scales[:, b, rows],
-                        rhs=m_codes[:, b, cols].bitcast(E4M3),
-                        rhs_scale=m_scales[:, b, cols],
-                        start=(b == 0),
-                        stop=(b == B - 1),
-                    )
-                if drains[t]:
-                    nc.vector.tensor_copy(out=dst[:, t, :], in_=bank[:])
-                else:
-                    nc.scalar.copy(out=dst[:, t, :], in_=bank[:])
-            nc.sync.dma_start(
-                out=out_1[256 * pair : 256 * (pair + 1), cols].rearrange("(t p) c -> p t c", t=2),
-                in_=dst[:],
+            rows = slice(128 * et, 128 * (et + 1))
+            nc.tensor.matmul_mx(
+                out=bank[:],
+                lhsT=go_codes[:, b, rows].bitcast(E5M2),
+                lhsT_scale=go_scales[:, b, rows],
+                rhs=m_codes[:, b, cols].bitcast(E4M3),
+                rhs_scale=m_scales[:, b, cols],
+                start=(b == 0),
+                stop=(b == B - 1),
             )
 
-        t00 = transpose_go(0, 0)
-        i00 = interleave(go_raw[0], 0)
-        t01 = transpose_go(0, 1)
-        i01 = interleave(go_raw[0], 1)
+        def out1_drains(banks, hh, on_vector, pairs):
+            for pair in pairs:
+                dst = stage.tile([P, 2, N], F32)
+                for t in range(2):
+                    if 2 * pair + t in on_vector:
+                        nc.vector.tensor_copy(out=dst[:, t, :], in_=banks[2 * pair + t][:])
+                    else:
+                        nc.scalar.copy(out=dst[:, t, :], in_=banks[2 * pair + t][:])
+                nc.sync.dma_start(
+                    out=out_1[
+                        256 * pair : 256 * (pair + 1), 512 * hh : 512 * (hh + 1)
+                    ].rearrange("(t p) c -> p t c", t=2),
+                    in_=dst[:],
+                )
+
+        t00, t01 = transpose_go(0)
+        i00 = interleave(nc.vector.tensor_copy, go_raw[0], 0)
+        i01 = interleave(nc.vector.tensor_copy, go_raw[0], 1)
+        gates = bank_tile()
+        nc.tensor.matmul(gates[:, :H], lhsT=ones[:], rhs=gate_sb[:], start=True, stop=True)
+        nc.vector.tensor_scalar(out=gate_lo[:], in0=gates[:, :H], scalar1=-40.0, scalar2=None, op0=ALU.max)
+        nc.scalar.activation(out=g_sb[:], in_=gates[:, :H], func=ACT.Sigmoid)
+        nc.scalar.activation(out=g_lo[:], in_=gate_lo[:], func=ACT.Sigmoid)
+        nc.scalar.activation(out=omg_sb[:], in_=gate_lo[:], func=ACT.Sigmoid, scale=-1.0)
         q_got(t00, 0, 0)
-        q_go(i00, 0, 0)
         q_got(t01, 0, 1)
-        q_go(i01, 0, 1)
-        for h in range(H):
-            gated_qkv(0, h)
-        w00 = interleave(wo_raw[0], 0)
-        w01 = interleave(wo_raw[0], 1)
+        w00 = interleave(nc.vector.tensor_copy, wo_raw[0], 0)
+        w01 = interleave(nc.scalar.copy, wo_raw[0], 1)
+        nc.vector.reciprocal(out=g_inv[:], in_=g_lo[:])
         q_wo(w00, 0, 0)
+        nc.vector.tensor_tensor(out=ratio[:], in0=omg_sb[:], in1=g_inv[:], op=ALU.mult)
+        q_go(i00, 0, 0)
         q_wo(w01, 0, 1)
-        t10 = transpose_go(1, 0)
-        t11 = transpose_go(1, 1)
-        w10 = interleave(wo_raw[1], 0)
-        w11 = interleave(wo_raw[1], 1)
+        q_go(i01, 0, 1)
+        t10, t11 = transpose_go(1)
+        w10 = interleave(nc.vector.tensor_copy, wo_raw[1], 0)
+        w11 = interleave(nc.scalar.copy, wo_raw[1], 1)
+        i10 = interleave(nc.vector.tensor_copy, go_raw[1], 0)
         q_wo(w10, 1, 0)
         q_wo(w11, 1, 1)
-        for h in range(4):
-            gated_qkv(1, h)
+        out0_group(0, 0, ())
         q_got(t10, 1, 0)
         q_got(t11, 1, 1)
-        i10 = interleave(go_raw[1], 0)
-        out0_group(0, 0)
-        i11 = interleave(go_raw[1], 1)
-        out0_group(0, 1)
+        out0_group(0, 1, ())
+        i11 = interleave(nc.vector.tensor_copy, go_raw[1], 1)
+        for h in range(4):
+            add_qkv(0, h)
         q_go(i10, 1, 0)
         q_go(i11, 1, 1)
-        for h in range(4, H):
-            gated_qkv(1, h)
         m00 = inter_tile()
         for h in range(4):
             merge(m00, 0, h)
-        out0_group(1, 0)
+        out0_group(1, 0, (3,))
+        for h in range(4):
+            add_qkv(1, h)
+        q_m(m00, 0, 0)
         m10 = inter_tile()
         for h in range(4):
             merge(m10, 1, h)
-        q_m(m00, 0, 0)
+        out0_group(1, 1, (1, 3))
+        for h in range(4, H):
+            add_qkv(0, h)
         q_m(m10, 1, 0)
-        out0_group(1, 1)
         m01 = inter_tile()
         for h in range(4, H):
             merge(m01, 0, h)
-        for pair in range(4):
-            out1_pair(0, pair, (False, False))
+        banks0 = []
+        for et in range(8):
+            bank = bank_tile()
+            for b in range(B):
+                out1_pass(bank, 0, et, b)
+            banks0.append(bank)
+        for h in range(4, H):
+            add_qkv(1, h)
+        q_m(m01, 0, 1)
         m11 = inter_tile()
+        out1_drains(banks0, 0, (1, 3, 5, 7), range(4))
         for h in range(4, H):
             merge(m11, 1, h)
-        q_m(m01, 0, 1)
         q_m(m11, 1, 1)
-        for pair in range(4):
-            out1_pair(1, pair, (False, True))
+        out1_drains(banks0, 0, (1, 3, 5, 7), range(4, 4))
+        banks1 = []
+        for et in range(8):
+            bank = bank_tile()
+            out1_pass(bank, 1, et, 0)
+            banks1.append(bank)
+        for et in range(8):
+            out1_pass(banks1[et], 1, et, 1)
+        out1_drains(banks1, 1, (1, 3, 5, 7), range(4))

@@ -33,7 +33,7 @@ def tile_knnxlmultiheadsattention_pb_v_kernel(
         const = ctx.enter_context(tc.tile_pool(name="const", bufs=1))
         keep = ctx.enter_context(tc.tile_pool(name="keep", bufs=1))
         raws = ctx.enter_context(tc.tile_pool(name="raws", bufs=4))
-        inter = ctx.enter_context(tc.tile_pool(name="inter", bufs=6))
+        inter = ctx.enter_context(tc.tile_pool(name="inter", bufs=14))
         stage = ctx.enter_context(tc.tile_pool(name="stage", bufs=8))
         psum = ctx.enter_context(tc.psum_pool(name="psum", bufs=8))
 
@@ -67,8 +67,8 @@ def tile_knnxlmultiheadsattention_pb_v_kernel(
 
         def load_go(b, lo, hi):
             nc.sync.dma_start(
-                out=go_raw[b][:, lo:hi, :],
-                in_=grad_out[b].rearrange("(p j) e -> p j e", j=PACK)[:, lo:hi, :],
+                out=go_raw[b][:, :, lo:hi],
+                in_=grad_out[b].rearrange("(p j) e -> p j e", j=PACK)[:, :, lo:hi],
             )
 
         def load_wo(g):
@@ -87,14 +87,14 @@ def tile_knnxlmultiheadsattention_pb_v_kernel(
         nc.vector.memset(ones[:], 1.0)
         nc.scalar.dma_start(out=gate_sb[0:1, :], in_=gate.rearrange("h a b -> (a b) h"))
         go_raw = [raw_tile()]
-        load_go(0, 0, 2)
-        load_go(0, 2, 4)
         wo_raw = [raw_tile()]
-        load_wo(0)
         go_raw.append(raw_tile())
-        load_go(1, 0, 4)
         wo_raw.append(raw_tile())
+        load_go(0, 0, 512)
+        load_wo(0)
+        load_go(0, 512, 1024)
         load_wo(1)
+        load_go(1, 0, 1024)
         for hh in range(2):
             for b in range(B):
                 load_heads(qkv_raw, qkv, b, 4 * hh, 4 * hh + 4)
@@ -108,9 +108,9 @@ def tile_knnxlmultiheadsattention_pb_v_kernel(
             bank = psum.tile([P, N], F32, tag="bank")
             return bank
 
-        def transpose_go(b):
-            grouped = [inter_tile(), inter_tile()]
-            for half, g in ((0, 0), (0, 1), (1, 0), (1, 1)):
+        def transpose_go(b, g):
+            grouped = inter_tile()
+            for half in range(2):
                 bank = bank_tile()
                 for jj in range(2):
                     words = go_raw[b][:, 2 * half + jj, :].bitcast(F32)
@@ -122,7 +122,7 @@ def tile_knnxlmultiheadsattention_pb_v_kernel(
                             ident[:],
                         )
                 nc.scalar.copy(
-                    out=grouped[g][:, 1024 * half : 1024 * (half + 1)]
+                    out=grouped[:, 1024 * half : 1024 * (half + 1)]
                     .bitcast(F32)
                     .rearrange("p (j r u) -> p j r u", j=2, u=2),
                     in_=bank[:].rearrange("p (j u r) -> p j r u", j=2, u=2),
@@ -213,14 +213,13 @@ def tile_knnxlmultiheadsattention_pb_v_kernel(
                 in_=dst[:],
             )
 
-        def out0_group(b, hh, on_vector):
+        def out0_products(b, hh):
+            return [out0_matmul(b, hh, j) for j in range(4)]
+
+        def out0_drains(drain, banks, b, hh):
             dst = raws.tile([P, 4, PACK * D], F32, tag="raw", align_bytes=64)
-            banks = [out0_matmul(b, hh, j) for j in range(4)]
             for j in range(4):
-                if j in on_vector:
-                    out0_drain_vector(banks[j], dst, hh, j)
-                else:
-                    out0_drain_scalar(banks[j], dst, hh, j)
+                drain(banks[j], dst, hh, j)
             out0_store(dst, b, hh)
 
         def out1_pass(bank, hh, et, b):
@@ -236,92 +235,103 @@ def tile_knnxlmultiheadsattention_pb_v_kernel(
                 stop=(b == B - 1),
             )
 
-        def out1_drains(banks, hh, on_vector, pairs):
-            for pair in pairs:
-                dst = stage.tile([P, 2, N], F32)
-                for t in range(2):
-                    if 2 * pair + t in on_vector:
-                        nc.vector.tensor_copy(out=dst[:, t, :], in_=banks[2 * pair + t][:])
-                    else:
-                        nc.scalar.copy(out=dst[:, t, :], in_=banks[2 * pair + t][:])
-                nc.sync.dma_start(
-                    out=out_1[
-                        256 * pair : 256 * (pair + 1), 512 * hh : 512 * (hh + 1)
-                    ].rearrange("(t p) c -> p t c", t=2),
-                    in_=dst[:],
-                )
+        def out1_products(hh, ets, b):
+            for et in ets:
+                if b == 0:
+                    out1_banks[hh, et] = bank_tile()
+                out1_pass(out1_banks[hh, et], hh, et, b)
 
-        t00, t01 = transpose_go(0)
-        i00 = interleave(nc.vector.tensor_copy, go_raw[0], 0)
-        i01 = interleave(nc.vector.tensor_copy, go_raw[0], 1)
+        out1_banks = {}
+
+        def out1_drains(hh, pair):
+            dst = stage.tile([P, 2, N], F32)
+            nc.scalar.copy(out=dst[:, 0, :], in_=out1_banks[hh, 2 * pair][:])
+            nc.vector.tensor_copy(out=dst[:, 1, :], in_=out1_banks[hh, 2 * pair + 1][:])
+            nc.sync.dma_start(
+                out=out_1[256 * pair : 256 * (pair + 1), 512 * hh : 512 * (hh + 1)].rearrange(
+                    "(t p) c -> p t c", t=2
+                ),
+                in_=dst[:],
+            )
+
+        on_v = nc.vector.tensor_copy
+        on_s = nc.scalar.copy
+        t00 = transpose_go(0, 0)
+        i00 = interleave(on_v, go_raw[0], 0)
         gates = bank_tile()
         nc.tensor.matmul(gates[:, :H], lhsT=ones[:], rhs=gate_sb[:], start=True, stop=True)
         nc.vector.tensor_scalar(out=gate_lo[:], in0=gates[:, :H], scalar1=-40.0, scalar2=None, op0=ALU.max)
         nc.scalar.activation(out=g_sb[:], in_=gates[:, :H], func=ACT.Sigmoid)
         nc.scalar.activation(out=g_lo[:], in_=gate_lo[:], func=ACT.Sigmoid)
         nc.scalar.activation(out=omg_sb[:], in_=gate_lo[:], func=ACT.Sigmoid, scale=-1.0)
-        q_got(t00, 0, 0)
-        q_got(t01, 0, 1)
-        w00 = interleave(nc.vector.tensor_copy, wo_raw[0], 0)
-        w01 = interleave(nc.scalar.copy, wo_raw[0], 1)
+        w00 = interleave(on_s, wo_raw[0], 0)
+        q_go(i00, 0, 0)
+        w01 = interleave(on_v, wo_raw[0], 1)
+        t01 = transpose_go(0, 1)
+        i01 = interleave(on_v, go_raw[0], 1)
         nc.vector.reciprocal(out=g_inv[:], in_=g_lo[:])
         q_wo(w00, 0, 0)
         nc.vector.tensor_tensor(out=ratio[:], in0=omg_sb[:], in1=g_inv[:], op=ALU.mult)
-        q_go(i00, 0, 0)
-        q_wo(w01, 0, 1)
+        w10 = interleave(on_s, wo_raw[1], 0)
+        w11 = interleave(on_v, wo_raw[1], 1)
         q_go(i01, 0, 1)
-        t10, t11 = transpose_go(1)
-        w10 = interleave(nc.vector.tensor_copy, wo_raw[1], 0)
-        w11 = interleave(nc.scalar.copy, wo_raw[1], 1)
-        i10 = interleave(nc.vector.tensor_copy, go_raw[1], 0)
-        q_wo(w10, 1, 0)
+        q_wo(w01, 0, 1)
         q_wo(w11, 1, 1)
-        out0_group(0, 0, ())
+        i10 = interleave(on_s, go_raw[1], 0)
+        q_got(t01, 0, 1)
+        q_wo(w10, 1, 0)
+        q_got(t00, 0, 0)
+        t10 = transpose_go(1, 0)
+        t11 = transpose_go(1, 1)
         q_got(t10, 1, 0)
-        q_got(t11, 1, 1)
-        out0_group(0, 1, ())
-        i11 = interleave(nc.vector.tensor_copy, go_raw[1], 1)
-        for h in range(4):
+        o00 = out0_products(0, 0)
+        for h in range(2):
             add_qkv(0, h)
-        q_go(i10, 1, 0)
-        q_go(i11, 1, 1)
+        q_got(t11, 1, 1)
+        for h in range(2, 4):
+            add_qkv(0, h)
+        o10 = out0_products(1, 0)
+        i11 = interleave(on_s, go_raw[1], 1)
+        out0_drains(out0_drain_vector, o00, 0, 0)
         m00 = inter_tile()
         for h in range(4):
             merge(m00, 0, h)
-        out0_group(1, 0, (3,))
+        o11 = out0_products(1, 1)
         for h in range(4):
             add_qkv(1, h)
+        out0_drains(out0_drain_scalar, o10, 1, 0)
+        o01 = out0_products(0, 1)
         q_m(m00, 0, 0)
+        q_go(i10, 1, 0)
         m10 = inter_tile()
         for h in range(4):
             merge(m10, 1, h)
-        out0_group(1, 1, (1, 3))
-        for h in range(4, H):
+        for h in range(4, 6):
             add_qkv(0, h)
+        out0_drains(out0_drain_vector, o11, 1, 1)
+        q_go(i11, 1, 1)
         q_m(m10, 1, 0)
+        out0_drains(out0_drain_scalar, o01, 0, 1)
+        for h in range(6, H):
+            add_qkv(0, h)
+        for et in range(8):
+            out1_products(0, (et,), 0)
+            out1_products(0, (et,), 1)
         m01 = inter_tile()
         for h in range(4, H):
             merge(m01, 0, h)
-        banks0 = []
-        for et in range(8):
-            bank = bank_tile()
-            for b in range(B):
-                out1_pass(bank, 0, et, b)
-            banks0.append(bank)
         for h in range(4, H):
             add_qkv(1, h)
+        out1_drains(0, 0)
+        out1_drains(0, 1)
         q_m(m01, 0, 1)
         m11 = inter_tile()
-        out1_drains(banks0, 0, (1, 3, 5, 7), range(4))
         for h in range(4, H):
             merge(m11, 1, h)
+        out1_drains(0, 2)
+        out1_drains(0, 3)
         q_m(m11, 1, 1)
-        out1_drains(banks0, 0, (1, 3, 5, 7), range(4, 4))
-        banks1 = []
-        for et in range(8):
-            bank = bank_tile()
-            out1_pass(bank, 1, et, 0)
-            banks1.append(bank)
-        for et in range(8):
-            out1_pass(banks1[et], 1, et, 1)
-        out1_drains(banks1, 1, (1, 3, 5, 7), range(4))
+        out1_products(1, range(8), 0)
+        out1_products(1, range(8), 1)
+        for pair in range(4):
+            out1_drains(1, pair)

@@ -34,7 +34,7 @@ def tile_knnxlmultiheadsattention_pb_v_kernel(
         keep = ctx.enter_context(tc.tile_pool(name="keep", bufs=1))
         raws = ctx.enter_context(tc.tile_pool(name="raws", bufs=4))
         inter = ctx.enter_context(tc.tile_pool(name="inter", bufs=14))
-        stage = ctx.enter_context(tc.tile_pool(name="stage", bufs=8))
+        stage = ctx.enter_context(tc.tile_pool(name="stage", bufs=4))
         psum = ctx.enter_context(tc.psum_pool(name="psum", bufs=8))
 
         gate_sb = const.tile([P, H], BF16)
@@ -46,6 +46,8 @@ def tile_knnxlmultiheadsattention_pb_v_kernel(
         omg_sb = const.tile([P, H], F32)
         ratio = const.tile([P, H], F32)
         ident = const.tile([P, P], F32)
+        nc.gpsimd.memset(gate_sb[:], 0.0)
+        nc.gpsimd.memset(ones[:], 1.0)
         make_identity(nc, ident[:])
 
         qkv_raw = keep.tile([P, B, H, PACK * D], BF16)
@@ -65,10 +67,9 @@ def tile_knnxlmultiheadsattention_pb_v_kernel(
             raw = raws.tile([P, PACK, 1024], BF16, tag="raw", align_bytes=64)
             return raw
 
-        def load_go(b, lo, hi):
+        def load_go(b):
             nc.sync.dma_start(
-                out=go_raw[b][:, :, lo:hi],
-                in_=grad_out[b].rearrange("(p j) e -> p j e", j=PACK)[:, :, lo:hi],
+                out=go_raw[b][:], in_=grad_out[b].rearrange("(p j) e -> p j e", j=PACK)
             )
 
         def load_wo(g):
@@ -83,18 +84,15 @@ def tile_knnxlmultiheadsattention_pb_v_kernel(
                 in_=src[b, lo:hi].rearrange("h (p j) d -> p h (j d)", j=PACK),
             )
 
-        nc.vector.memset(gate_sb[:], 0.0)
-        nc.vector.memset(ones[:], 1.0)
-        nc.scalar.dma_start(out=gate_sb[0:1, :], in_=gate.rearrange("h a b -> (a b) h"))
+        nc.sync.dma_start(out=gate_sb[0:1, :], in_=gate.rearrange("h a b -> (a b) h"))
         go_raw = [raw_tile()]
         wo_raw = [raw_tile()]
         go_raw.append(raw_tile())
         wo_raw.append(raw_tile())
-        load_go(0, 0, 512)
+        load_go(0)
         load_wo(0)
-        load_go(0, 512, 1024)
+        load_go(1)
         load_wo(1)
-        load_go(1, 0, 1024)
         for hh in range(2):
             for b in range(B):
                 load_heads(qkv_raw, qkv, b, 4 * hh, 4 * hh + 4)
@@ -138,6 +136,18 @@ def tile_knnxlmultiheadsattention_pb_v_kernel(
                 out=grouped[:].rearrange("p (c i j) -> p c j i", i=4, j=PACK),
                 in_=raw[:, :, 512 * half : 512 * (half + 1)].rearrange("p j (c i) -> p c j i", i=4),
             )
+            return grouped
+
+        def interleave_go(copy, b, half):
+            grouped = inter_tile()
+            for k in range(2):
+                cols = slice(512 * half + 256 * k, 512 * half + 256 * (k + 1))
+                copy(
+                    out=grouped[:, 1024 * k : 1024 * (k + 1)].rearrange(
+                        "p (t c m j) -> p c j m t", t=2, m=2, j=PACK
+                    ),
+                    in_=go_raw[b][:, :, cols].rearrange("p j (c m t) -> p c j m t", t=2, m=2),
+                )
             return grouped
 
         def q_got(grouped, b, g):
@@ -216,122 +226,111 @@ def tile_knnxlmultiheadsattention_pb_v_kernel(
         def out0_products(b, hh):
             return [out0_matmul(b, hh, j) for j in range(4)]
 
-        def out0_drains(drain, banks, b, hh):
+        def out0_drains(vector_js, banks, b, hh):
             dst = raws.tile([P, 4, PACK * D], F32, tag="raw", align_bytes=64)
             for j in range(4):
+                drain = out0_drain_vector if j in vector_js else out0_drain_scalar
                 drain(banks[j], dst, hh, j)
             out0_store(dst, b, hh)
 
-        def out1_pass(bank, hh, et, b):
+        def out1_product(hh, et):
+            bank = bank_tile()
             cols = slice(512 * hh, 512 * (hh + 1))
             rows = slice(128 * et, 128 * (et + 1))
-            nc.tensor.matmul_mx(
-                out=bank[:],
-                lhsT=go_codes[:, b, rows].bitcast(E5M2),
-                lhsT_scale=go_scales[:, b, rows],
-                rhs=m_codes[:, b, cols].bitcast(E4M3),
-                rhs_scale=m_scales[:, b, cols],
-                start=(b == 0),
-                stop=(b == B - 1),
-            )
+            for b in range(B):
+                nc.tensor.matmul_mx(
+                    out=bank[:],
+                    lhsT=go_codes[:, b, rows].bitcast(E5M2),
+                    lhsT_scale=go_scales[:, b, rows],
+                    rhs=m_codes[:, b, cols].bitcast(E4M3),
+                    rhs_scale=m_scales[:, b, cols],
+                    start=(b == 0),
+                    stop=(b == B - 1),
+                )
+            return bank
 
-        def out1_products(hh, ets, b):
-            for et in ets:
-                if b == 0:
-                    out1_banks[hh, et] = bank_tile()
-                out1_pass(out1_banks[hh, et], hh, et, b)
+        def out1_drain(copy, bank, rows, hh, t):
+            copy(out=rows[:, t, 512 * hh : 512 * (hh + 1)], in_=bank[:])
 
-        out1_banks = {}
-
-        def out1_drains(hh, pair):
-            dst = stage.tile([P, 2, N], F32)
-            nc.scalar.copy(out=dst[:, 0, :], in_=out1_banks[hh, 2 * pair][:])
-            nc.vector.tensor_copy(out=dst[:, 1, :], in_=out1_banks[hh, 2 * pair + 1][:])
+        def out1_store(rows, k):
             nc.sync.dma_start(
-                out=out_1[256 * pair : 256 * (pair + 1), 512 * hh : 512 * (hh + 1)].rearrange(
-                    "(t p) c -> p t c", t=2
-                ),
-                in_=dst[:],
+                out=out_1[256 * k : 256 * (k + 1), :].rearrange("(m t) c -> m t c", t=2),
+                in_=rows[:],
             )
 
         on_v = nc.vector.tensor_copy
         on_s = nc.scalar.copy
-        t00 = transpose_go(0, 0)
-        i00 = interleave(on_v, go_raw[0], 0)
         gates = bank_tile()
         nc.tensor.matmul(gates[:, :H], lhsT=ones[:], rhs=gate_sb[:], start=True, stop=True)
         nc.vector.tensor_scalar(out=gate_lo[:], in0=gates[:, :H], scalar1=-40.0, scalar2=None, op0=ALU.max)
         nc.scalar.activation(out=g_sb[:], in_=gates[:, :H], func=ACT.Sigmoid)
         nc.scalar.activation(out=g_lo[:], in_=gate_lo[:], func=ACT.Sigmoid)
         nc.scalar.activation(out=omg_sb[:], in_=gate_lo[:], func=ACT.Sigmoid, scale=-1.0)
-        w00 = interleave(on_s, wo_raw[0], 0)
-        q_go(i00, 0, 0)
-        w01 = interleave(on_v, wo_raw[0], 1)
-        t01 = transpose_go(0, 1)
-        i01 = interleave(on_v, go_raw[0], 1)
         nc.vector.reciprocal(out=g_inv[:], in_=g_lo[:])
-        q_wo(w00, 0, 0)
         nc.vector.tensor_tensor(out=ratio[:], in0=omg_sb[:], in1=g_inv[:], op=ALU.mult)
-        w10 = interleave(on_s, wo_raw[1], 0)
-        w11 = interleave(on_v, wo_raw[1], 1)
-        q_go(i01, 0, 1)
-        q_wo(w01, 0, 1)
-        q_wo(w11, 1, 1)
-        i10 = interleave(on_s, go_raw[1], 0)
-        q_got(t01, 0, 1)
-        q_wo(w10, 1, 0)
+        t00 = transpose_go(0, 0)
+        t01 = transpose_go(0, 1)
+        i00 = interleave_go(on_v, 0, 0)
+        i01 = interleave_go(on_v, 0, 1)
         q_got(t00, 0, 0)
+        q_go(i00, 0, 0)
+        q_got(t01, 0, 1)
+        w00 = interleave(on_s, wo_raw[0], 0)
+        w01 = interleave(on_v, wo_raw[0], 1)
+        q_go(i01, 0, 1)
+        q_wo(w00, 0, 0)
+        q_wo(w01, 0, 1)
         t10 = transpose_go(1, 0)
         t11 = transpose_go(1, 1)
+        w10 = interleave(on_s, wo_raw[1], 0)
+        i10 = interleave_go(on_s, 1, 0)
+        w11 = interleave(on_v, wo_raw[1], 1)
         q_got(t10, 1, 0)
-        o00 = out0_products(0, 0)
-        for h in range(2):
-            add_qkv(0, h)
+        q_wo(w11, 1, 1)
         q_got(t11, 1, 1)
-        for h in range(2, 4):
-            add_qkv(0, h)
+        q_wo(w10, 1, 0)
+        o00 = out0_products(0, 0)
         o10 = out0_products(1, 0)
-        i11 = interleave(on_s, go_raw[1], 1)
-        out0_drains(out0_drain_vector, o00, 0, 0)
+        i11 = interleave_go(on_s, 1, 1)
+        for h in range(4):
+            add_qkv(0, h)
+        out0_drains(range(4), o00, 0, 0)
         m00 = inter_tile()
         for h in range(4):
             merge(m00, 0, h)
         o11 = out0_products(1, 1)
         for h in range(4):
             add_qkv(1, h)
-        out0_drains(out0_drain_scalar, o10, 1, 0)
+        q_go(i10, 1, 0)
+        out0_drains((3,), o10, 1, 0)
         o01 = out0_products(0, 1)
         q_m(m00, 0, 0)
-        q_go(i10, 1, 0)
         m10 = inter_tile()
         for h in range(4):
             merge(m10, 1, h)
-        for h in range(4, 6):
+        for h in range(4, H):
             add_qkv(0, h)
-        out0_drains(out0_drain_vector, o11, 1, 1)
+        out0_drains(range(4), o11, 1, 1)
         q_go(i11, 1, 1)
         q_m(m10, 1, 0)
-        out0_drains(out0_drain_scalar, o01, 0, 1)
-        for h in range(6, H):
-            add_qkv(0, h)
-        for et in range(8):
-            out1_products(0, (et,), 0)
-            out1_products(0, (et,), 1)
         m01 = inter_tile()
         for h in range(4, H):
             merge(m01, 0, h)
+        out0_drains((), o01, 0, 1)
         for h in range(4, H):
             add_qkv(1, h)
-        out1_drains(0, 0)
-        out1_drains(0, 1)
         q_m(m01, 0, 1)
         m11 = inter_tile()
         for h in range(4, H):
             merge(m11, 1, h)
-        out1_drains(0, 2)
-        out1_drains(0, 3)
         q_m(m11, 1, 1)
-        out1_products(1, range(8), 0)
-        out1_products(1, range(8), 1)
-        for pair in range(4):
-            out1_drains(1, pair)
+        for k in range(4):
+            rows = stage.tile([P, 2, HD], F32)
+            banks = {}
+            for hh in range(2):
+                for t in range(2):
+                    banks[hh, t] = out1_product(hh, 2 * k + t)
+            for hh in range(2):
+                for t in range(2):
+                    out1_drain(on_v if t else on_s, banks[hh, t], rows, hh, t)
+            out1_store(rows, k)

from contextlib import ExitStack

import concourse.mybir as mybir
from concourse.masks import make_identity

B, S, E, H, D = 2, 512, 1024, 8, 128
HD = H * D
T = B * S
FLOPS = 2 * 2 * T * E * HD
BYTES = 2 * (T * E + E * HD + T * HD + H) + 4 * T * HD + 4 * (T * HD + E * HD)

F32 = mybir.dt.float32
BF16 = mybir.dt.bfloat16
U32 = mybir.dt.uint32
U8 = mybir.dt.uint8
E4M3 = mybir.dt.float8_e4m3fn_x4
E5M2 = mybir.dt.float8_e5m2_x4
ACT = mybir.ActivationFunctionType
ALU = mybir.AluOpType

P = 128
PACK = 4
N = 512
WIDE = N * PACK


def tile_knnxlmultiheadsattention_pb_v_kernel(
    tc, q, qkv, kv_external, gate, Wo, bo, qkv_ext, grad_out, out_0, out_1
):
    nc = tc.nc

    with ExitStack() as ctx:
        const = ctx.enter_context(tc.tile_pool(name="const", bufs=1))
        keep = ctx.enter_context(tc.tile_pool(name="keep", bufs=1))
        raws = ctx.enter_context(tc.tile_pool(name="raws", bufs=4))
        inter = ctx.enter_context(tc.tile_pool(name="inter", bufs=14))
        stage = ctx.enter_context(tc.tile_pool(name="stage", bufs=4))
        psum = ctx.enter_context(tc.psum_pool(name="psum", bufs=8))

        gate_sb = const.tile([P, H], BF16)
        ones = const.tile([P, P], BF16)
        g_sb = const.tile([P, H], F32)
        gate_lo = const.tile([P, H], F32)
        g_lo = const.tile([P, H], F32)
        g_inv = const.tile([P, H], F32)
        omg_sb = const.tile([P, H], F32)
        ratio = const.tile([P, H], F32)
        ident = const.tile([P, P], F32)
        nc.gpsimd.memset(gate_sb[:], 0.0)
        nc.gpsimd.memset(ones[:], 1.0)
        make_identity(nc, ident[:])

        qkv_raw = keep.tile([P, B, H, PACK * D], BF16)
        ext_raw = keep.tile([P, B, H, PACK * D], F32)
        got_codes = keep.tile([P, B * 2, N], U32, align_bytes=64)
        got_scales = keep.tile([P, B * 2, N], U8, align_bytes=64)
        go_codes = keep.tile([P, B, E], U32, align_bytes=64)
        go_scales = keep.tile([P, B, E], U8, align_bytes=64)
        wo_codes = keep.tile([P, 2, HD], U32, align_bytes=64)
        wo_scales = keep.tile([P, 2, HD], U8, align_bytes=64)
        m_codes = keep.tile([P, B, HD], U32, align_bytes=64)
        m_scales = keep.tile([P, B, HD], U8, align_bytes=64)

        ctx.enter_context(tc.manual_schedule())

        def raw_tile():
            raw = raws.tile([P, PACK, 1024], BF16, tag="raw", align_bytes=64)
            return raw

        def load_go(b):
            nc.sync.dma_start(
                out=go_raw[b][:], in_=grad_out[b].rearrange("(p j) e -> p j e", j=PACK)
            )

        def load_wo(g):
            nc.sync.dma_start(
                out=wo_raw[g][:],
                in_=Wo[512 * g : 512 * (g + 1), :].rearrange("(p j) c -> p j c", j=PACK),
            )

        def load_heads(dst, src, b, lo, hi):
            nc.sync.dma_start(
                out=dst[:, b, lo:hi, :],
                in_=src[b, lo:hi].rearrange("h (p j) d -> p h (j d)", j=PACK),
            )

        nc.sync.dma_start(out=gate_sb[0:1, :], in_=gate.rearrange("h a b -> (a b) h"))
        go_raw = [raw_tile()]
        wo_raw = [raw_tile()]
        go_raw.append(raw_tile())
        wo_raw.append(raw_tile())
        load_go(0)
        load_wo(0)
        load_go(1)
        load_wo(1)
        for hh in range(2):
            for b in range(B):
                load_heads(qkv_raw, qkv, b, 4 * hh, 4 * hh + 4)
                load_heads(ext_raw, qkv_ext, b, 4 * hh, 4 * hh + 4)

        def inter_tile():
            grouped = inter.tile([P, WIDE], BF16, tag="grouped", align_bytes=64)
            return grouped

        def bank_tile():
            bank = psum.tile([P, N], F32, tag="bank")
            return bank

        def transpose_go(b, g):
            grouped = inter_tile()
            for half in range(2):
                bank = bank_tile()
                for jj in range(2):
                    words = go_raw[b][:, 2 * half + jj, :].bitcast(F32)
                    for u in range(2):
                        c0 = 128 * (2 * jj + u)
                        nc.tensor.transpose(
                            bank[:, c0 : c0 + 128],
                            words[:, 256 * g + u : 256 * (g + 1) : 2],
                            ident[:],
                        )
                nc.scalar.copy(
                    out=grouped[:, 1024 * half : 1024 * (half + 1)]
                    .bitcast(F32)
                    .rearrange("p (j r u) -> p j r u", j=2, u=2),
                    in_=bank[:].rearrange("p (j u r) -> p j r u", j=2, u=2),
                )
            return grouped

        def quant(grouped, codes, scales, fmt):
            nc.vector.quantize_mx(out=codes.bitcast(fmt), scales=scales, in_=grouped[:])

        def interleave(copy, raw, half):
            grouped = inter_tile()
            copy(
                out=grouped[:].rearrange("p (c i j) -> p c j i", i=4, j=PACK),
                in_=raw[:, :, 512 * half : 512 * (half + 1)].rearrange("p j (c i) -> p c j i", i=4),
            )
            return grouped

        def interleave_go(copy, b, half):
            grouped = inter_tile()
            for k in range(2):
                cols = slice(512 * half + 256 * k, 512 * half + 256 * (k + 1))
                copy(
                    out=grouped[:, 1024 * k : 1024 * (k + 1)].rearrange(
                        "p (t c m j) -> p c j m t", t=2, m=2, j=PACK
                    ),
                    in_=go_raw[b][:, :, cols].rearrange("p j (c m t) -> p c j m t", t=2, m=2),
                )
            return grouped

        def q_got(grouped, b, g):
            quant(grouped, got_codes[:, 2 * b + g, :], got_scales[:, 2 * b + g, :], E5M2)

        def q_go(grouped, b, half):
            cols = slice(512 * half, 512 * (half + 1))
            quant(grouped, go_codes[:, b, cols], go_scales[:, b, cols], E5M2)

        def q_wo(grouped, g, half):
            cols = slice(512 * half, 512 * (half + 1))
            quant(grouped, wo_codes[:, g, cols], wo_scales[:, g, cols], E4M3)

        def q_m(grouped, b, half):
            cols = slice(512 * half, 512 * (half + 1))
            quant(grouped, m_codes[:, b, cols], m_scales[:, b, cols], E4M3)

        def add_qkv(b, h):
            nc.vector.scalar_tensor_tensor(
                out=ext_raw[:, b, h, :],
                in0=ext_raw[:, b, h, :],
                scalar=ratio[:, h : h + 1],
                in1=qkv_raw[:, b, h, :],
                op0=ALU.mult,
                op1=ALU.add,
            )

        def merge(grouped, b, h):
            lo = D * PACK * (h % 4)
            nc.scalar.activation(
                out=grouped[:, lo : lo + D * PACK].rearrange("p (c i j) -> p c j i", i=4, j=PACK),
                in_=ext_raw[:, b, h, :].rearrange("p (j c i) -> p c j i", i=4, j=PACK),
                func=ACT.Copy,
                scale=g_lo[:, h : h + 1],
            )

        def out0_matmul(b, hh, j):
            bank = bank_tile()
            cols = slice(512 * hh, 512 * (hh + 1))
            toks = slice(128 * j, 128 * (j + 1))
            for g in range(2):
                nc.tensor.matmul_mx(
                    out=bank[:],
                    lhsT=got_codes[:, 2 * b + g, toks].bitcast(E5M2),
                    lhsT_scale=got_scales[:, 2 * b + g, toks],
                    rhs=wo_codes[:, g, cols].bitcast(E4M3),
                    rhs_scale=wo_scales[:, g, cols],
                    start=(g == 0),
                    stop=(g == 1),
                )
            return bank

        def out0_drain_scalar(bank, dst, hh, j):
            for h in range(4):
                nc.scalar.activation(
                    out=dst[:, h, 128 * j : 128 * (j + 1)],
                    in_=bank[:, 128 * h : 128 * (h + 1)],
                    func=ACT.Copy,
                    scale=g_sb[:, 4 * hh + h : 4 * hh + h + 1],
                )

        def out0_drain_vector(bank, dst, hh, j):
            nc.vector.tensor_tensor(
                out=dst[:, :, 128 * j : 128 * (j + 1)],
                in0=bank[:].rearrange("p (h d) -> p h d", h=4),
                in1=g_sb[:, 4 * hh : 4 * hh + 4].unsqueeze(2).to_broadcast([P, 4, D]),
                op=ALU.mult,
            )

        def out0_store(dst, b, hh):
            nc.sync.dma_start(
                out=out_0[b, 4 * hh : 4 * hh + 4].rearrange("h (p j) d -> p h (j d)", j=PACK),
                in_=dst[:],
            )

        def out0_products(b, hh):
            return [out0_matmul(b, hh, j) for j in range(4)]

        def out0_drains(vector_js, banks, b, hh):
            dst = raws.tile([P, 4, PACK * D], F32, tag="raw", align_bytes=64)
            for j in range(4):
                drain = out0_drain_vector if j in vector_js else out0_drain_scalar
                drain(banks[j], dst, hh, j)
            out0_store(dst, b, hh)

        def out1_product(hh, et):
            bank = bank_tile()
            cols = slice(512 * hh, 512 * (hh + 1))
            rows = slice(128 * et, 128 * (et + 1))
            for b in range(B):
                nc.tensor.matmul_mx(
                    out=bank[:],
                    lhsT=go_codes[:, b, rows].bitcast(E5M2),
                    lhsT_scale=go_scales[:, b, rows],
                    rhs=m_codes[:, b, cols].bitcast(E4M3),
                    rhs_scale=m_scales[:, b, cols],
                    start=(b == 0),
                    stop=(b == B - 1),
                )
            return bank

        def out1_drain(copy, bank, rows, hh, t):
            copy(out=rows[:, t, 512 * hh : 512 * (hh + 1)], in_=bank[:])

        def out1_store(rows, k):
            nc.sync.dma_start(
                out=out_1[256 * k : 256 * (k + 1), :].rearrange("(m t) c -> m t c", t=2),
                in_=rows[:],
            )

        on_v = nc.vector.tensor_copy
        on_s = nc.scalar.copy
        gates = bank_tile()
        nc.tensor.matmul(gates[:, :H], lhsT=ones[:], rhs=gate_sb[:], start=True, stop=True)
        nc.vector.tensor_scalar(out=gate_lo[:], in0=gates[:, :H], scalar1=-40.0, scalar2=None, op0=ALU.max)
        nc.scalar.activation(out=g_sb[:], in_=gates[:, :H], func=ACT.Sigmoid)
        nc.scalar.activation(out=g_lo[:], in_=gate_lo[:], func=ACT.Sigmoid)
        nc.scalar.activation(out=omg_sb[:], in_=gate_lo[:], func=ACT.Sigmoid, scale=-1.0)
        nc.vector.reciprocal(out=g_inv[:], in_=g_lo[:])
        nc.vector.tensor_tensor(out=ratio[:], in0=omg_sb[:], in1=g_inv[:], op=ALU.mult)
        t00 = transpose_go(0, 0)
        t01 = transpose_go(0, 1)
        i00 = interleave_go(on_v, 0, 0)
        i01 = interleave_go(on_v, 0, 1)
        q_got(t00, 0, 0)
        q_go(i00, 0, 0)
        q_got(t01, 0, 1)
        w00 = interleave(on_s, wo_raw[0], 0)
        w01 = interleave(on_v, wo_raw[0], 1)
        q_go(i01, 0, 1)
        q_wo(w00, 0, 0)
        q_wo(w01, 0, 1)
        t10 = transpose_go(1, 0)
        t11 = transpose_go(1, 1)
        w10 = interleave(on_s, wo_raw[1], 0)
        i10 = interleave_go(on_s, 1, 0)
        w11 = interleave(on_v, wo_raw[1], 1)
        q_got(t10, 1, 0)
        q_wo(w11, 1, 1)
        q_got(t11, 1, 1)
        q_wo(w10, 1, 0)
        o00 = out0_products(0, 0)
        o10 = out0_products(1, 0)
        i11 = interleave_go(on_s, 1, 1)
        for h in range(4):
            add_qkv(0, h)
        out0_drains(range(4), o00, 0, 0)
        m00 = inter_tile()
        for h in range(4):
            merge(m00, 0, h)
        o11 = out0_products(1, 1)
        for h in range(4):
            add_qkv(1, h)
        q_go(i10, 1, 0)
        out0_drains((3,), o10, 1, 0)
        o01 = out0_products(0, 1)
        q_m(m00, 0, 0)
        m10 = inter_tile()
        for h in range(4):
            merge(m10, 1, h)
        for h in range(4, H):
            add_qkv(0, h)
        out0_drains(range(4), o11, 1, 1)
        q_go(i11, 1, 1)
        q_m(m10, 1, 0)
        m01 = inter_tile()
        for h in range(4, H):
            merge(m01, 0, h)
        out0_drains((), o01, 0, 1)
        for h in range(4, H):
            add_qkv(1, h)
        q_m(m01, 0, 1)
        m11 = inter_tile()
        for h in range(4, H):
            merge(m11, 1, h)
        q_m(m11, 1, 1)
        for k in range(4):
            rows = stage.tile([P, 2, HD], F32)
            banks = {}
            for hh in range(2):
                for t in range(2):
                    banks[hh, t] = out1_product(hh, 2 * k + t)
            for hh in range(2):
                for t in range(2):
                    out1_drain(on_v if t else on_s, banks[hh, t], rows, hh, t)
            out1_store(rows, k)
